import numpy as np
import ml_dtypes


def mxq(x, axis, fmt="e4m3"):
    dtype, down = {"e4m3": (ml_dtypes.float8_e4m3fn, 7), "e5m2": (ml_dtypes.float8_e5m2, 14)}[fmt]
    v = np.moveaxis(np.asarray(x, np.float32).astype(ml_dtypes.bfloat16).astype(np.float64), axis, -1)
    blocks = v.reshape(v.shape[:-1] + (-1, 32))
    amax = np.abs(blocks).max(-1, keepdims=True)
    byte = np.maximum(np.where(amax > 0, np.frexp(amax)[1] - 1 + 127, 0) - down, 1)
    scale = np.exp2(byte - 127.0)
    codes = (blocks / scale).astype(np.float32).astype(dtype).astype(np.float64)
    return np.moveaxis((codes * scale).reshape(v.shape), -1, axis)


WIDE = False


def mx_kscale(k):
    if not WIDE:
        return np.ones(k)
    levels = np.array([10, -10, 5, -5, 0])
    if k % 512:
        return np.exp2(np.random.permutation(np.resize(levels, k // 32))).repeat(32)
    a = np.empty((k // 512, 16))
    for p in range(k // 512):
        a[p, :8] = np.random.permutation(np.resize(levels, 8))
        for g in range(8):
            far = levels[np.abs(levels - a[p, g]) >= 10]
            a[p, g + 8] = far[np.random.randint(len(far))]
    return np.exp2(a.ravel()).repeat(32)


BF16 = ml_dtypes.bfloat16


def bf(x):
    return np.asarray(x, np.float32).astype(BF16)


def f64(x):
    return np.asarray(x).astype(np.float64)


B, N0, N1, N2, N3, T, K = 128, 512, 512, 512, 512, 1, 512
R = min(K, N0, N1)
R2 = min(R, T)
GS = 0.25


def setup_inputs():
    s, t = mx_kscale(R), mx_kscale(R)
    return {"S": bf(np.random.standard_normal((R, R, R2)) * s[:, None, None] * t[None, :, None]),
            "U0": bf(np.random.standard_normal((N1, R)) / np.sqrt(R) / s[None, :]),
            "U1": bf(np.random.standard_normal((N0, R)) * GS / np.sqrt(R) / t[None, :])}


def reference(S, U0, U1):
    w1 = mxq(f64(S).reshape(R, R * R2).T, 1, "e4m3") @ mxq(f64(U0).T, 0, "e4m3")
    w2 = mxq(w1.reshape(R, R2 * N1).T, 1, "e4m3") @ mxq(f64(U1).T, 0, "e4m3")
    return w2.reshape(R2, N1, N0)

@@ -1,0 +1,166 @@
+from contextlib import ExitStack
+
+import concourse.mybir as mybir
+from concourse.masks import make_identity
+
+BF16 = mybir.dt.bfloat16
+F32 = mybir.dt.float32
+U32 = mybir.dt.uint32
+U8 = mybir.dt.uint8
+FP8X4 = mybir.dt.float8_e4m3fn_x4
+
+P = 128
+PACK = 4
+DIM = 512
+HALF = DIM // 2
+BLOCKS = DIM // P
+RUN = 4
+WARM_MATMULS = 6
+
+FLOPS = 2 * 2 * DIM * DIM * DIM
+
+
+def empty_bank(nc, on_vector, out, in_):
+    if on_vector:
+        nc.vector.tensor_copy(out=out, in_=in_)
+    else:
+        nc.scalar.copy(out=out, in_=in_)
+
+
+def quantise(nc, codes, scales, cols, values):
+    nc.vector.quantize_mx(out=codes[:, cols].bitcast(FP8X4), scales=scales[:, cols], in_=values)
+
+
+def load_factor(nc, pool, factor, name):
+    rows = pool.tile([P, 2, 2 * DIM], BF16, name=name)
+    for h in range(2):
+        nc.sync.dma_start(
+            out=rows[:, h, :],
+            in_=factor[h * HALF : (h + 1) * HALF, :].rearrange("(r b) k -> r (b k)", b=2),
+        )
+    return rows
+
+
+def idle_matmul(nc, idle_bank, identity):
+    nc.tensor.matmul(out=idle_bank[:], lhsT=identity[:], rhs=identity[:], start=True, stop=True)
+
+
+def transpose_half(nc, psum, rows, h, identity, name):
+    words = rows[:, h, :].bitcast(F32)
+    bank = psum.tile([P, PACK, P], F32, tag="bank", name="%s_bank%d" % (name, h))
+    for b in range(2):
+        for u in range(2):
+            every_second = words[:, b * HALF + u : (b + 1) * HALF : 2]
+            nc.tensor.transpose(bank[:, 2 * b + u, :], every_second, identity[:])
+    return bank
+
+
+def quantise_factor(nc, pool, banks, vector_takes_last, name):
+    codes = pool.tile([P, DIM], U32, name=name + "_codes", align_bytes=64)
+    scales = pool.tile([P, DIM], U8, name=name + "_scales", align_bytes=64)
+    grouped = []
+    for h in range(2):
+        values = pool.tile([P, HALF * PACK], BF16, name="%s_grouped%d" % (name, h), align_bytes=64)
+        empty_bank(
+            nc,
+            vector_takes_last and h == 1,
+            out=values[:].bitcast(F32).rearrange("w (r s) -> w r s", s=PACK),
+            in_=banks[h][:].rearrange("w s r -> w r s"),
+        )
+        grouped.append(values)
+        if h == 1:
+            quantise(nc, codes, scales, slice(0, HALF), grouped[0][:])
+    quantise(nc, codes, scales, slice(HALF, DIM), grouped[1][:])
+    return codes, scales
+
+
+def tile_mtl_net_tf_pa_s_kernel(tc, S, U0, U1, out):
+    nc = tc.nc
+    with ExitStack() as ctx:
+        ctx.enter_context(tc.manual_schedule())
+        keep = ctx.enter_context(tc.tile_pool(name="keep", bufs=1))
+        psum = ctx.enter_context(tc.psum_pool(name="psum", bufs=8))
+
+        identity = keep.tile([P, P], F32)
+        make_identity(nc, identity[:])
+
+        s_rows = keep.tile([P, PACK, DIM], BF16)
+        nc.sync.dma_start(
+            out=s_rows[:].rearrange("w t p -> w (t p)"),
+            in_=S.rearrange("(w t) p r -> w (t p r)", t=PACK),
+        )
+        u0_rows = load_factor(nc, keep, U0, "u0_rows")
+        u1_rows = load_factor(nc, keep, U1, "u1_rows")
+
+        idle_bank = psum.tile([P, P], F32, tag="bank")
+        for n in range(WARM_MATMULS):
+            idle_matmul(nc, idle_bank, identity)
+
+        u0_banks = []
+        u1_banks = []
+        for h in range(2):
+            u0_banks.append(transpose_half(nc, psum, u0_rows, h, identity, "u0"))
+            idle_matmul(nc, idle_bank, identity)
+        for h in range(2):
+            u1_banks.append(transpose_half(nc, psum, u1_rows, h, identity, "u1"))
+            if h == 0:
+                idle_matmul(nc, idle_bank, identity)
+
+        s_grouped = keep.tile([P, DIM, PACK], BF16, align_bytes=64)
+        s_codes = keep.tile([P, DIM], U32, align_bytes=64)
+        s_scales = keep.tile([P, DIM], U8, align_bytes=64)
+        s_from = s_rows[:].rearrange("w t (c i e) -> w e c t i", i=RUN, e=PACK)
+        s_to = s_grouped[:].rearrange("w (e c i) t -> w e c t i", e=PACK, i=RUN)
+        s_values = s_grouped[:].rearrange("w c t -> w (c t)")
+        for e in range(PACK):
+            nc.vector.tensor_copy(out=s_to[:, e], in_=s_from[:, e])
+            if e == PACK - 1:
+                quantise(nc, s_codes, s_scales, slice(0, HALF), s_values[:, 0 : HALF * PACK])
+        quantise(nc, s_codes, s_scales, slice(HALF, DIM), s_values[:, HALF * PACK : DIM * PACK])
+
+        u0_codes, u0_scales = quantise_factor(nc, keep, u0_banks, False, "u0")
+        u1_codes, u1_scales = quantise_factor(nc, keep, u1_banks, True, "u1")
+
+        w1_banks = []
+        for jb in range(BLOCKS):
+            j_cols = slice(jb * P, (jb + 1) * P)
+            w1_bank = psum.tile([P, PACK, P], F32, tag="bank", name="w1_bank%d" % jb)
+            for t in range(PACK):
+                p_cols = slice(t * P, (t + 1) * P)
+                nc.tensor.matmul_mx(
+                    out=w1_bank[:, t, :],
+                    lhsT=s_codes[:, p_cols].bitcast(FP8X4),
+                    lhsT_scale=s_scales[:, p_cols],
+                    rhs=u0_codes[:, j_cols].bitcast(FP8X4),
+                    rhs_scale=u0_scales[:, j_cols],
+                    start=True,
+                    stop=True,
+                )
+            w1_banks.append(w1_bank)
+
+        w1_codes = keep.tile([P, DIM], U32, align_bytes=64)
+        w1_scales = keep.tile([P, DIM], U8, align_bytes=64)
+        w1_grouped = []
+        for jb in range(BLOCKS):
+            values = keep.tile([P, P, PACK], BF16, name="w1_grouped%d" % jb, align_bytes=64)
+            empty_bank(nc, jb == BLOCKS - 1, out=values[:], in_=w1_banks[jb][:].rearrange("c t j -> c j t"))
+            w1_grouped.append(values[:].rearrange("c j t -> c (j t)"))
+            if jb > 0:
+                quantise(nc, w1_codes, w1_scales, slice((jb - 1) * P, jb * P), w1_grouped[jb - 1])
+        quantise(nc, w1_codes, w1_scales, slice(DIM - P, DIM), w1_grouped[BLOCKS - 1])
+
+        for jb in range(BLOCKS):
+            j_cols = slice(jb * P, (jb + 1) * P)
+            out_bank = psum.tile([P, DIM], F32, tag="bank", name="out_bank%d" % jb)
+            nc.tensor.matmul_mx(
+                out=out_bank[:],
+                lhsT=w1_codes[:, j_cols].bitcast(FP8X4),
+                lhsT_scale=w1_scales[:, j_cols],
+                rhs=u1_codes[:].bitcast(FP8X4),
+                rhs_scale=u1_scales[:],
+                start=True,
+                stop=True,
+            )
+            out_rows = keep.tile([P, DIM], F32, name="out_rows%d" % jb)
+            empty_bank(nc, jb == BLOCKS - 1, out=out_rows[:], in_=out_bank[:])
+            nc.sync.dma_start(out=out[0, j_cols, :], in_=out_rows[:])

@@ -15,7 +15,6 @@ DIM = 512
 HALF = DIM // 2
 BLOCKS = DIM // P
 RUN = 4
-WARM_MATMULS = 6
 
 FLOPS = 2 * 2 * DIM * DIM * DIM
 
@@ -31,22 +30,21 @@ def quantise(nc, codes, scales, cols, values):
     nc.vector.quantize_mx(out=codes[:, cols].bitcast(FP8X4), scales=scales[:, cols], in_=values)
 
 
-def load_factor(nc, pool, factor, name):
-    rows = pool.tile([P, 2, 2 * DIM], BF16, name=name)
-    for h in range(2):
-        nc.sync.dma_start(
-            out=rows[:, h, :],
-            in_=factor[h * HALF : (h + 1) * HALF, :].rearrange("(r b) k -> r (b k)", b=2),
-        )
+def load_half(nc, pool, factor, h, name):
+    rows = pool.tile([P, 2 * DIM], BF16, name="%s_rows%d" % (name, h))
+    nc.sync.dma_start(
+        out=rows[:],
+        in_=factor[h * HALF : (h + 1) * HALF, :].rearrange("(r b) k -> r (b k)", b=2),
+    )
     return rows
 
 
-def idle_matmul(nc, idle_bank, identity):
-    nc.tensor.matmul(out=idle_bank[:], lhsT=identity[:], rhs=identity[:], start=True, stop=True)
+def idle_matmul(nc, idle_bank, zeros):
+    nc.tensor.matmul(out=idle_bank[:], lhsT=zeros[:], rhs=zeros[:], start=True, stop=True)
 
 
 def transpose_half(nc, psum, rows, h, identity, name):
-    words = rows[:, h, :].bitcast(F32)
+    words = rows[:].bitcast(F32)
     bank = psum.tile([P, PACK, P], F32, tag="bank", name="%s_bank%d" % (name, h))
     for b in range(2):
         for u in range(2):
@@ -55,23 +53,15 @@ def transpose_half(nc, psum, rows, h, identity, name):
     return bank
 
 
-def quantise_factor(nc, pool, banks, vector_takes_last, name):
-    codes = pool.tile([P, DIM], U32, name=name + "_codes", align_bytes=64)
-    scales = pool.tile([P, DIM], U8, name=name + "_scales", align_bytes=64)
-    grouped = []
-    for h in range(2):
-        values = pool.tile([P, HALF * PACK], BF16, name="%s_grouped%d" % (name, h), align_bytes=64)
-        empty_bank(
-            nc,
-            vector_takes_last and h == 1,
-            out=values[:].bitcast(F32).rearrange("w (r s) -> w r s", s=PACK),
-            in_=banks[h][:].rearrange("w s r -> w r s"),
-        )
-        grouped.append(values)
-        if h == 1:
-            quantise(nc, codes, scales, slice(0, HALF), grouped[0][:])
-    quantise(nc, codes, scales, slice(HALF, DIM), grouped[1][:])
-    return codes, scales
+def regroup_half(nc, pool, bank, on_vector, name):
+    values = pool.tile([P, HALF * PACK], BF16, name=name, align_bytes=64)
+    empty_bank(
+        nc,
+        on_vector,
+        out=values[:].bitcast(F32).rearrange("w (r s) -> w r s", s=PACK),
+        in_=bank[:].rearrange("w s r -> w r s"),
+    )
+    return values
 
 
 def tile_mtl_net_tf_pa_s_kernel(tc, S, U0, U1, out):
@@ -81,6 +71,8 @@ def tile_mtl_net_tf_pa_s_kernel(tc, S, U0, U1, out):
         keep = ctx.enter_context(tc.tile_pool(name="keep", bufs=1))
         psum = ctx.enter_context(tc.psum_pool(name="psum", bufs=8))
 
+        idle_operand = keep.tile([P, P], F32)
+        nc.vector.memset(idle_operand[:], 0.0)
         identity = keep.tile([P, P], F32)
         make_identity(nc, identity[:])
 
@@ -89,46 +81,49 @@ def tile_mtl_net_tf_pa_s_kernel(tc, S, U0, U1, out):
             out=s_rows[:].rearrange("w t p -> w (t p)"),
             in_=S.rearrange("(w t) p r -> w (t p r)", t=PACK),
         )
-        u0_rows = load_factor(nc, keep, U0, "u0_rows")
-        u1_rows = load_factor(nc, keep, U1, "u1_rows")
-
-        idle_bank = psum.tile([P, P], F32, tag="bank")
-        for n in range(WARM_MATMULS):
-            idle_matmul(nc, idle_bank, identity)
-
-        u0_banks = []
-        u1_banks = []
-        for h in range(2):
-            u0_banks.append(transpose_half(nc, psum, u0_rows, h, identity, "u0"))
-            idle_matmul(nc, idle_bank, identity)
-        for h in range(2):
-            u1_banks.append(transpose_half(nc, psum, u1_rows, h, identity, "u1"))
-            if h == 0:
-                idle_matmul(nc, idle_bank, identity)
+        u0_rows = [load_half(nc, keep, U0, h, "u0") for h in range(2)]
+        u1_rows = [load_half(nc, keep, U1, h, "u1") for h in range(2)]
 
         s_grouped = keep.tile([P, DIM, PACK], BF16, align_bytes=64)
         s_codes = keep.tile([P, DIM], U32, align_bytes=64)
         s_scales = keep.tile([P, DIM], U8, align_bytes=64)
+        u0_codes = keep.tile([P, DIM], U32, align_bytes=64)
+        u0_scales = keep.tile([P, DIM], U8, align_bytes=64)
+        u1_codes = keep.tile([P, DIM], U32, align_bytes=64)
+        u1_scales = keep.tile([P, DIM], U8, align_bytes=64)
+        w1_codes = keep.tile([P, DIM], U32, align_bytes=64)
+        w1_scales = keep.tile([P, DIM], U8, align_bytes=64)
+        half_cols = (slice(0, HALF), slice(HALF, DIM))
+
+        idle_bank = psum.tile([P, P], F32, tag="bank")
+
+        def idle(count):
+            for n in range(count):
+                idle_matmul(nc, idle_bank, idle_operand)
+
+        def transposes(rows, h, name):
+            return transpose_half(nc, psum, rows[h], h, identity, name)
+
+        def regroup(bank, h, on_vector, name):
+            return regroup_half(nc, keep, bank, on_vector, "%s_grouped%d" % (name, h))
+
         s_from = s_rows[:].rearrange("w t (c i e) -> w e c t i", i=RUN, e=PACK)
         s_to = s_grouped[:].rearrange("w (e c i) t -> w e c t i", e=PACK, i=RUN)
         s_values = s_grouped[:].rearrange("w c t -> w (c t)")
-        for e in range(PACK):
-            nc.vector.tensor_copy(out=s_to[:, e], in_=s_from[:, e])
-            if e == PACK - 1:
-                quantise(nc, s_codes, s_scales, slice(0, HALF), s_values[:, 0 : HALF * PACK])
-        quantise(nc, s_codes, s_scales, slice(HALF, DIM), s_values[:, HALF * PACK : DIM * PACK])
 
-        u0_codes, u0_scales = quantise_factor(nc, keep, u0_banks, False, "u0")
-        u1_codes, u1_scales = quantise_factor(nc, keep, u1_banks, True, "u1")
+        def regroup_s(e, on_vector):
+            empty_bank(nc, on_vector, out=s_to[:, e], in_=s_from[:, e])
 
-        w1_banks = []
-        for jb in range(BLOCKS):
+        def quantise_s(h):
+            quantise(nc, s_codes, s_scales, half_cols[h], s_values[:, h * HALF * PACK : (h + 1) * HALF * PACK])
+
+        def first_contraction(jb):
             j_cols = slice(jb * P, (jb + 1) * P)
-            w1_bank = psum.tile([P, PACK, P], F32, tag="bank", name="w1_bank%d" % jb)
+            bank = psum.tile([P, PACK, P], F32, tag="bank", name="w1_bank%d" % jb)
             for t in range(PACK):
                 p_cols = slice(t * P, (t + 1) * P)
                 nc.tensor.matmul_mx(
-                    out=w1_bank[:, t, :],
+                    out=bank[:, t, :],
                     lhsT=s_codes[:, p_cols].bitcast(FP8X4),
                     lhsT_scale=s_scales[:, p_cols],
                     rhs=u0_codes[:, j_cols].bitcast(FP8X4),
@@ -136,31 +131,80 @@ def tile_mtl_net_tf_pa_s_kernel(tc, S, U0, U1, out):
                     start=True,
                     stop=True,
                 )
-            w1_banks.append(w1_bank)
+            return bank
 
-        w1_codes = keep.tile([P, DIM], U32, align_bytes=64)
-        w1_scales = keep.tile([P, DIM], U8, align_bytes=64)
-        w1_grouped = []
-        for jb in range(BLOCKS):
+        def regroup_w1(jb, bank, on_vector):
             values = keep.tile([P, P, PACK], BF16, name="w1_grouped%d" % jb, align_bytes=64)
-            empty_bank(nc, jb == BLOCKS - 1, out=values[:], in_=w1_banks[jb][:].rearrange("c t j -> c j t"))
-            w1_grouped.append(values[:].rearrange("c j t -> c (j t)"))
-            if jb > 0:
-                quantise(nc, w1_codes, w1_scales, slice((jb - 1) * P, jb * P), w1_grouped[jb - 1])
-        quantise(nc, w1_codes, w1_scales, slice(DIM - P, DIM), w1_grouped[BLOCKS - 1])
+            empty_bank(nc, on_vector, out=values[:], in_=bank[:].rearrange("c t j -> c j t"))
+            return values[:].rearrange("c j t -> c (j t)")
 
-        for jb in range(BLOCKS):
+        def quantise_w1(jb, values):
+            quantise(nc, w1_codes, w1_scales, slice(jb * P, (jb + 1) * P), values)
+
+        def second_contraction(jb, cols):
+            bank = psum.tile([P, DIM], F32, tag="bank", name="out_bank%d_%d" % (jb, cols.start))
+            bank = bank[:, 0 : cols.stop - cols.start]
             j_cols = slice(jb * P, (jb + 1) * P)
-            out_bank = psum.tile([P, DIM], F32, tag="bank", name="out_bank%d" % jb)
             nc.tensor.matmul_mx(
-                out=out_bank[:],
+                out=bank,
                 lhsT=w1_codes[:, j_cols].bitcast(FP8X4),
                 lhsT_scale=w1_scales[:, j_cols],
-                rhs=u1_codes[:].bitcast(FP8X4),
-                rhs_scale=u1_scales[:],
+                rhs=u1_codes[:, cols].bitcast(FP8X4),
+                rhs_scale=u1_scales[:, cols],
                 start=True,
                 stop=True,
             )
-            out_rows = keep.tile([P, DIM], F32, name="out_rows%d" % jb)
-            empty_bank(nc, jb == BLOCKS - 1, out=out_rows[:], in_=out_bank[:])
-            nc.sync.dma_start(out=out[0, j_cols, :], in_=out_rows[:])
+            return bank
+
+        def store(jb, cols, bank, on_vector):
+            width = cols.stop - cols.start
+            rows = keep.tile([P, width], F32, name="out_rows%d_%d" % (jb, cols.start))
+            empty_bank(nc, on_vector, out=rows[:], in_=bank)
+            nc.sync.dma_start(out=out[0, jb * P : (jb + 1) * P, cols], in_=rows[:])
+
+        whole = slice(0, DIM)
+
+        idle(6)
+        for e in range(PACK):
+            regroup_s(e, True)
+        quantise_s(0)
+
+        u0_bank0 = transposes(u0_rows, 0, "u0")
+        idle(0)
+        u0_first = regroup(u0_bank0, 0, False, "u0")
+        u0_bank1 = transposes(u0_rows, 1, "u0")
+        idle(1)
+        u0_second = regroup(u0_bank1, 1, False, "u0")
+        quantise(nc, u0_codes, u0_scales, half_cols[0], u0_first[:])
+        quantise_s(1)
+        u1_bank0 = transposes(u1_rows, 0, "u1")
+        idle(1)
+        u1_first = regroup(u1_bank0, 0, False, "u1")
+        quantise(nc, u0_codes, u0_scales, half_cols[1], u0_second[:])
+        u1_bank1 = transposes(u1_rows, 1, "u1")
+
+        bank0 = first_contraction(0)
+        bank1 = first_contraction(1)
+        bank2 = first_contraction(2)
+        bank3 = first_contraction(3)
+        quantise(nc, u1_codes, u1_scales, half_cols[0], u1_first[:])
+        u1_second = regroup(u1_bank1, 1, False, "u1")
+        w1_0 = regroup_w1(0, bank0, True)
+        w1_1 = regroup_w1(1, bank1, False)
+        quantise(nc, u1_codes, u1_scales, half_cols[1], u1_second[:])
+        quantise_w1(0, w1_0)
+        quantise_w1(1, w1_1)
+        w1_3 = regroup_w1(3, bank3, True)
+        w1_2 = regroup_w1(2, bank2, False)
+        quantise_w1(2, w1_2)
+
+        out0 = second_contraction(0, whole)
+        out1 = second_contraction(1, whole)
+        out2 = second_contraction(2, whole)
+        store(0, whole, out0, False)
+        quantise_w1(3, w1_3)
+        out3 = [second_contraction(3, cols) for cols in half_cols]
+        store(1, whole, out1, True)
+        store(2, whole, out2, False)
+        store(3, half_cols[0], out3[0], True)
+        store(3, half_cols[1], out3[1], False)

@@ -203,8 +203,7 @@ def tile_mtl_net_tf_pa_s_kernel(tc, S, U0, U1, out):
         out2 = second_contraction(2, whole)
         store(0, whole, out0, False)
         quantise_w1(3, w1_3)
-        out3 = [second_contraction(3, cols) for cols in half_cols]
+        out3 = second_contraction(3, whole)
         store(1, whole, out1, True)
         store(2, whole, out2, False)
-        store(3, half_cols[0], out3[0], True)
-        store(3, half_cols[1], out3[1], False)
+        store(3, whole, out3, True)

@@ -76,12 +76,13 @@ def tile_mtl_net_tf_pa_s_kernel(tc, S, U0, U1, out):
         identity = keep.tile([P, P], F32)
         make_identity(nc, identity[:])
 
+        u0_rows = [load_half(nc, keep, U0, 0, "u0")]
         s_rows = keep.tile([P, PACK, DIM], BF16)
         nc.sync.dma_start(
             out=s_rows[:].rearrange("w t p -> w (t p)"),
             in_=S.rearrange("(w t) p r -> w (t p r)", t=PACK),
         )
-        u0_rows = [load_half(nc, keep, U0, h, "u0") for h in range(2)]
+        u0_rows.append(load_half(nc, keep, U0, 1, "u0"))
         u1_rows = [load_half(nc, keep, U1, h, "u1") for h in range(2)]
 
         s_grouped = keep.tile([P, DIM, PACK], BF16, align_bytes=64)
@@ -164,19 +165,20 @@ def tile_mtl_net_tf_pa_s_kernel(tc, S, U0, U1, out):
 
         whole = slice(0, DIM)
 
-        idle(6)
-        for e in range(PACK):
-            regroup_s(e, True)
-        quantise_s(0)
-
+        idle(4)
         u0_bank0 = transposes(u0_rows, 0, "u0")
-        idle(0)
+        idle(3)
         u0_first = regroup(u0_bank0, 0, False, "u0")
+        regroup_s(0, True)
+        regroup_s(2, False)
+        regroup_s(1, True)
+        regroup_s(3, True)
+        quantise_s(0)
+        quantise(nc, u0_codes, u0_scales, half_cols[0], u0_first[:])
+        quantise_s(1)
         u0_bank1 = transposes(u0_rows, 1, "u0")
         idle(1)
         u0_second = regroup(u0_bank1, 1, False, "u0")
-        quantise(nc, u0_codes, u0_scales, half_cols[0], u0_first[:])
-        quantise_s(1)
         u1_bank0 = transposes(u1_rows, 0, "u1")
         idle(1)
         u1_first = regroup(u1_bank0, 0, False, "u1")

@@ -39,8 +39,8 @@ def load_half(nc, pool, factor, h, name):
     return rows
 
 
-def idle_matmul(nc, idle_bank, zeros):
-    nc.tensor.matmul(out=idle_bank[:], lhsT=zeros[:], rhs=zeros[:], start=True, stop=True)
+def idle_matmul(nc, idle_bank, ones):
+    nc.tensor.matmul(out=idle_bank[:], lhsT=ones[:], rhs=ones[:], start=True, stop=True)
 
 
 def transpose_half(nc, psum, rows, h, identity, name):
@@ -72,7 +72,7 @@ def tile_mtl_net_tf_pa_s_kernel(tc, S, U0, U1, out):
         psum = ctx.enter_context(tc.psum_pool(name="psum", bufs=8))
 
         idle_operand = keep.tile([P, P], F32)
-        nc.vector.memset(idle_operand[:], 0.0)
+        nc.vector.memset(idle_operand[:], 1.0)
         identity = keep.tile([P, P], F32)
         make_identity(nc, identity[:])
 

@@ -163,6 +163,15 @@ def tile_mtl_net_tf_pa_s_kernel(tc, S, U0, U1, out):
             empty_bank(nc, on_vector, out=rows[:], in_=bank)
             nc.sync.dma_start(out=out[0, jb * P : (jb + 1) * P, cols], in_=rows[:])
 
+        def store_pair(jb, banks):
+            rows = keep.tile([P, DIM], F32, name="out_pair%d" % jb)
+            for cols, bank, on_vector in zip(half_cols, banks, (False, True)):
+                empty_bank(nc, on_vector, out=rows[:, cols], in_=bank)
+            nc.sync.dma_start(out=out[0, jb * P : (jb + 1) * P, :], in_=rows[:])
+
+        def second_pair(jb):
+            return [second_contraction(jb, cols) for cols in half_cols]
+
         whole = slice(0, DIM)
 
         idle(4)
@@ -200,12 +209,12 @@ def tile_mtl_net_tf_pa_s_kernel(tc, S, U0, U1, out):
         w1_2 = regroup_w1(2, bank2, False)
         quantise_w1(2, w1_2)
 
-        out0 = second_contraction(0, whole)
-        out1 = second_contraction(1, whole)
-        out2 = second_contraction(2, whole)
-        store(0, whole, out0, False)
+        out0 = second_pair(0)
+        out1 = second_pair(1)
+        store_pair(0, out0)
+        out2 = second_pair(2)
+        store_pair(1, out1)
         quantise_w1(3, w1_3)
-        out3 = second_contraction(3, whole)
-        store(1, whole, out1, True)
-        store(2, whole, out2, False)
-        store(3, whole, out3, True)
+        out3 = second_pair(3)
+        store_pair(2, out2)
+        store_pair(3, out3)

@@ -176,17 +176,16 @@ def tile_mtl_net_tf_pa_s_kernel(tc, S, U0, U1, out):
 
         idle(4)
         u0_bank0 = transposes(u0_rows, 0, "u0")
-        idle(3)
-        u0_first = regroup(u0_bank0, 0, False, "u0")
+        idle(2)
         regroup_s(0, True)
         regroup_s(2, False)
+        u0_first = regroup(u0_bank0, 0, False, "u0")
         regroup_s(1, True)
         regroup_s(3, True)
         quantise_s(0)
-        quantise(nc, u0_codes, u0_scales, half_cols[0], u0_first[:])
         quantise_s(1)
+        quantise(nc, u0_codes, u0_scales, half_cols[0], u0_first[:])
         u0_bank1 = transposes(u0_rows, 1, "u0")
-        idle(1)
         u0_second = regroup(u0_bank1, 1, False, "u0")
         u1_bank0 = transposes(u1_rows, 0, "u1")
         idle(1)
@@ -205,8 +204,8 @@ def tile_mtl_net_tf_pa_s_kernel(tc, S, U0, U1, out):
         quantise(nc, u1_codes, u1_scales, half_cols[1], u1_second[:])
         quantise_w1(0, w1_0)
         quantise_w1(1, w1_1)
-        w1_3 = regroup_w1(3, bank3, True)
         w1_2 = regroup_w1(2, bank2, False)
+        w1_3 = regroup_w1(3, bank3, False)
         quantise_w1(2, w1_2)
 
         out0 = second_pair(0)

from contextlib import ExitStack

import concourse.mybir as mybir
from concourse.masks import make_identity

BF16 = mybir.dt.bfloat16
F32 = mybir.dt.float32
U32 = mybir.dt.uint32
U8 = mybir.dt.uint8
FP8X4 = mybir.dt.float8_e4m3fn_x4

P = 128
PACK = 4
DIM = 512
HALF = DIM // 2
BLOCKS = DIM // P
RUN = 4

FLOPS = 2 * 2 * DIM * DIM * DIM


def empty_bank(nc, on_vector, out, in_):
    if on_vector:
        nc.vector.tensor_copy(out=out, in_=in_)
    else:
        nc.scalar.copy(out=out, in_=in_)


def quantise(nc, codes, scales, cols, values):
    nc.vector.quantize_mx(out=codes[:, cols].bitcast(FP8X4), scales=scales[:, cols], in_=values)


def load_half(nc, pool, factor, h, name):
    rows = pool.tile([P, 2 * DIM], BF16, name="%s_rows%d" % (name, h))
    nc.sync.dma_start(
        out=rows[:],
        in_=factor[h * HALF : (h + 1) * HALF, :].rearrange("(r b) k -> r (b k)", b=2),
    )
    return rows


def idle_matmul(nc, idle_bank, ones):
    nc.tensor.matmul(out=idle_bank[:], lhsT=ones[:], rhs=ones[:], start=True, stop=True)


def transpose_half(nc, psum, rows, h, identity, name):
    words = rows[:].bitcast(F32)
    bank = psum.tile([P, PACK, P], F32, tag="bank", name="%s_bank%d" % (name, h))
    for b in range(2):
        for u in range(2):
            every_second = words[:, b * HALF + u : (b + 1) * HALF : 2]
            nc.tensor.transpose(bank[:, 2 * b + u, :], every_second, identity[:])
    return bank


def regroup_half(nc, pool, bank, on_vector, name):
    values = pool.tile([P, HALF * PACK], BF16, name=name, align_bytes=64)
    empty_bank(
        nc,
        on_vector,
        out=values[:].bitcast(F32).rearrange("w (r s) -> w r s", s=PACK),
        in_=bank[:].rearrange("w s r -> w r s"),
    )
    return values


def tile_mtl_net_tf_pa_s_kernel(tc, S, U0, U1, out):
    nc = tc.nc
    with ExitStack() as ctx:
        ctx.enter_context(tc.manual_schedule())
        keep = ctx.enter_context(tc.tile_pool(name="keep", bufs=1))
        psum = ctx.enter_context(tc.psum_pool(name="psum", bufs=8))

        idle_operand = keep.tile([P, P], F32)
        nc.vector.memset(idle_operand[:], 1.0)
        identity = keep.tile([P, P], F32)
        make_identity(nc, identity[:])

        u0_rows = [load_half(nc, keep, U0, 0, "u0")]
        s_rows = keep.tile([P, PACK, DIM], BF16)
        nc.sync.dma_start(
            out=s_rows[:].rearrange("w t p -> w (t p)"),
            in_=S.rearrange("(w t) p r -> w (t p r)", t=PACK),
        )
        u0_rows.append(load_half(nc, keep, U0, 1, "u0"))
        u1_rows = [load_half(nc, keep, U1, h, "u1") for h in range(2)]

        s_grouped = keep.tile([P, DIM, PACK], BF16, align_bytes=64)
        s_codes = keep.tile([P, DIM], U32, align_bytes=64)
        s_scales = keep.tile([P, DIM], U8, align_bytes=64)
        u0_codes = keep.tile([P, DIM], U32, align_bytes=64)
        u0_scales = keep.tile([P, DIM], U8, align_bytes=64)
        u1_codes = keep.tile([P, DIM], U32, align_bytes=64)
        u1_scales = keep.tile([P, DIM], U8, align_bytes=64)
        w1_codes = keep.tile([P, DIM], U32, align_bytes=64)
        w1_scales = keep.tile([P, DIM], U8, align_bytes=64)
        half_cols = (slice(0, HALF), slice(HALF, DIM))

        idle_bank = psum.tile([P, P], F32, tag="bank")

        def idle(count):
            for n in range(count):
                idle_matmul(nc, idle_bank, idle_operand)

        def transposes(rows, h, name):
            return transpose_half(nc, psum, rows[h], h, identity, name)

        def regroup(bank, h, on_vector, name):
            return regroup_half(nc, keep, bank, on_vector, "%s_grouped%d" % (name, h))

        s_from = s_rows[:].rearrange("w t (c i e) -> w e c t i", i=RUN, e=PACK)
        s_to = s_grouped[:].rearrange("w (e c i) t -> w e c t i", e=PACK, i=RUN)
        s_values = s_grouped[:].rearrange("w c t -> w (c t)")

        def regroup_s(e, on_vector):
            empty_bank(nc, on_vector, out=s_to[:, e], in_=s_from[:, e])

        def quantise_s(h):
            quantise(nc, s_codes, s_scales, half_cols[h], s_values[:, h * HALF * PACK : (h + 1) * HALF * PACK])

        def first_contraction(jb):
            j_cols = slice(jb * P, (jb + 1) * P)
            bank = psum.tile([P, PACK, P], F32, tag="bank", name="w1_bank%d" % jb)
            for t in range(PACK):
                p_cols = slice(t * P, (t + 1) * P)
                nc.tensor.matmul_mx(
                    out=bank[:, t, :],
                    lhsT=s_codes[:, p_cols].bitcast(FP8X4),
                    lhsT_scale=s_scales[:, p_cols],
                    rhs=u0_codes[:, j_cols].bitcast(FP8X4),
                    rhs_scale=u0_scales[:, j_cols],
                    start=True,
                    stop=True,
                )
            return bank

        def regroup_w1(jb, bank, on_vector):
            values = keep.tile([P, P, PACK], BF16, name="w1_grouped%d" % jb, align_bytes=64)
            empty_bank(nc, on_vector, out=values[:], in_=bank[:].rearrange("c t j -> c j t"))
            return values[:].rearrange("c j t -> c (j t)")

        def quantise_w1(jb, values):
            quantise(nc, w1_codes, w1_scales, slice(jb * P, (jb + 1) * P), values)

        def second_contraction(jb, cols):
            bank = psum.tile([P, DIM], F32, tag="bank", name="out_bank%d_%d" % (jb, cols.start))
            bank = bank[:, 0 : cols.stop - cols.start]
            j_cols = slice(jb * P, (jb + 1) * P)
            nc.tensor.matmul_mx(
                out=bank,
                lhsT=w1_codes[:, j_cols].bitcast(FP8X4),
                lhsT_scale=w1_scales[:, j_cols],
                rhs=u1_codes[:, cols].bitcast(FP8X4),
                rhs_scale=u1_scales[:, cols],
                start=True,
                stop=True,
            )
            return bank

        def store(jb, cols, bank, on_vector):
            width = cols.stop - cols.start
            rows = keep.tile([P, width], F32, name="out_rows%d_%d" % (jb, cols.start))
            empty_bank(nc, on_vector, out=rows[:], in_=bank)
            nc.sync.dma_start(out=out[0, jb * P : (jb + 1) * P, cols], in_=rows[:])

        def store_pair(jb, banks):
            rows = keep.tile([P, DIM], F32, name="out_pair%d" % jb)
            for cols, bank, on_vector in zip(half_cols, banks, (False, True)):
                empty_bank(nc, on_vector, out=rows[:, cols], in_=bank)
            nc.sync.dma_start(out=out[0, jb * P : (jb + 1) * P, :], in_=rows[:])

        def second_pair(jb):
            return [second_contraction(jb, cols) for cols in half_cols]

        whole = slice(0, DIM)

        idle(4)
        u0_bank0 = transposes(u0_rows, 0, "u0")
        idle(2)
        regroup_s(0, True)
        regroup_s(2, False)
        u0_first = regroup(u0_bank0, 0, False, "u0")
        regroup_s(1, True)
        regroup_s(3, True)
        quantise_s(0)
        quantise_s(1)
        quantise(nc, u0_codes, u0_scales, half_cols[0], u0_first[:])
        u0_bank1 = transposes(u0_rows, 1, "u0")
        u0_second = regroup(u0_bank1, 1, False, "u0")
        u1_bank0 = transposes(u1_rows, 0, "u1")
        idle(1)
        u1_first = regroup(u1_bank0, 0, False, "u1")
        quantise(nc, u0_codes, u0_scales, half_cols[1], u0_second[:])
        u1_bank1 = transposes(u1_rows, 1, "u1")

        bank0 = first_contraction(0)
        bank1 = first_contraction(1)
        bank2 = first_contraction(2)
        bank3 = first_contraction(3)
        quantise(nc, u1_codes, u1_scales, half_cols[0], u1_first[:])
        u1_second = regroup(u1_bank1, 1, False, "u1")
        w1_0 = regroup_w1(0, bank0, True)
        w1_1 = regroup_w1(1, bank1, False)
        quantise(nc, u1_codes, u1_scales, half_cols[1], u1_second[:])
        quantise_w1(0, w1_0)
        quantise_w1(1, w1_1)
        w1_2 = regroup_w1(2, bank2, False)
        w1_3 = regroup_w1(3, bank3, False)
        quantise_w1(2, w1_2)

        out0 = second_pair(0)
        out1 = second_pair(1)
        store_pair(0, out0)
        out2 = second_pair(2)
        store_pair(1, out1)
        quantise_w1(3, w1_3)
        out3 = second_pair(3)
        store_pair(2, out2)
        store_pair(3, out3)
